import numpy as np
import ml_dtypes


def mxq(x, axis, fmt="e4m3"):
    dtype, down = {"e4m3": (ml_dtypes.float8_e4m3fn, 7), "e5m2": (ml_dtypes.float8_e5m2, 14)}[fmt]
    v = np.moveaxis(np.asarray(x, np.float32).astype(ml_dtypes.bfloat16).astype(np.float64), axis, -1)
    blocks = v.reshape(v.shape[:-1] + (-1, 32))
    amax = np.abs(blocks).max(-1, keepdims=True)
    byte = np.maximum(np.where(amax > 0, np.frexp(amax)[1] - 1 + 127, 0) - down, 1)
    scale = np.exp2(byte - 127.0)
    codes = (blocks / scale).astype(np.float32).astype(dtype).astype(np.float64)
    return np.moveaxis((codes * scale).reshape(v.shape), -1, axis)


WIDE = False


def mx_kscale(k):
    if not WIDE:
        return np.ones(k)
    levels = np.array([10, -10, 5, -5, 0])
    if k % 512:
        return np.exp2(np.random.permutation(np.resize(levels, k // 32))).repeat(32)
    a = np.empty((k // 512, 16))
    for p in range(k // 512):
        a[p, :8] = np.random.permutation(np.resize(levels, 8))
        for g in range(8):
            far = levels[np.abs(levels - a[p, g]) >= 10]
            a[p, g + 8] = far[np.random.randint(len(far))]
    return np.exp2(a.ravel()).repeat(32)


BF16 = ml_dtypes.bfloat16


def bf(x):
    return np.asarray(x, np.float32).astype(BF16)


def f64(x):
    return np.asarray(x).astype(np.float64)


B, T, D, H = 8, 1024, 512, 128
N = B * T
EMA0 = 1.0


def sigmoid(v):
    return 1.0 / (1.0 + np.exp(-v))


def surprise_gate(err):
    err_mag = np.sqrt(np.sum(err * err)) / N
    ema = 0.95 * EMA0 + 0.05 * err_mag
    return np.minimum(err_mag / np.maximum(ema, 1e-8), 3.0)


def setup_inputs():
    s, t = mx_kscale(D), mx_kscale(N)
    return {"err": bf(np.random.standard_normal((N, D)) * 2.3 * s[None, :] * t[:, None]),
            "W_down": bf(np.random.standard_normal((D, H)) / np.sqrt(D) / s[:, None]),
            "gate_pre": bf(np.random.standard_normal((N, H))),
            "up_pre": bf(np.random.standard_normal((N, H))),
            "x_pred": bf(np.random.standard_normal((N, D)) / t[:, None])}


def reference(err, W_down, gate_pre, up_pre, x_pred):
    err, gate_pre, up_pre = f64(err), f64(gate_pre), f64(up_pre)
    sg = surprise_gate(err)
    d_h = mxq(err, 1, "e4m3") @ mxq(f64(W_down), 0, "e4m3")
    sig = sigmoid(gate_pre)
    gate_act = gate_pre * sig
    d_gate_act = d_h * up_pre
    d_up_val = d_h * gate_act
    d_gate_pre = d_gate_act * sig * (1.0 + gate_pre * (1.0 - sig))
    xq = mxq(f64(x_pred), 0, "e4m3")
    grad_gate = (mxq(d_gate_pre, 0, "e4m3").T @ xq) / N
    grad_up = (mxq(d_up_val, 0, "e4m3").T @ xq) / N
    return grad_up * sg, grad_gate * sg

@@ -1,0 +1,397 @@
+from contextlib import ExitStack
+
+import concourse.mybir as mybir
+from concourse.masks import make_identity
+
+F32 = mybir.dt.float32
+BF16 = mybir.dt.bfloat16
+U32 = mybir.dt.uint32
+U8 = mybir.dt.uint8
+FP8X4 = mybir.dt.float8_e4m3fn_x4
+ACT = mybir.ActivationFunctionType
+ALU = mybir.AluOpType
+
+P = 128
+PACK = 4
+K_PASS = P * PACK
+
+N_TOKENS = 8192
+D = 512
+H = 128
+N_CHUNKS = N_TOKENS // K_PASS
+
+FLOPS = 3 * 2 * N_TOKENS * D * H
+
+SCALAR_AHEAD = 3
+X_AHEAD = 2
+LOAD_AHEAD = 2
+SQUARES_LATE = 4
+GRAM = P
+X_SHARE = 128
+
+
+def tile_continuummemorysystem_pa_t_kernel(
+    tc, err, W_down, gate_pre, up_pre, x_pred, out_0, out_1
+):
+    nc = tc.nc
+    with ExitStack() as ctx:
+        const = ctx.enter_context(tc.tile_pool(name="const", bufs=1))
+        inputs = ctx.enter_context(
+            tc.tile_pool(name="inputs", bufs=LOAD_AHEAD + SCALAR_AHEAD + 2)
+        )
+        err_in = ctx.enter_context(
+            tc.tile_pool(name="err_in", bufs=LOAD_AHEAD + SQUARES_LATE + 2)
+        )
+        early = ctx.enter_context(tc.tile_pool(name="early", bufs=SCALAR_AHEAD + 1))
+        x_mx = ctx.enter_context(tc.tile_pool(name="x_mx", bufs=X_AHEAD + 2))
+        work = ctx.enter_context(tc.tile_pool(name="work", bufs=2))
+        psum_t = ctx.enter_context(tc.psum_pool(name="psum_t", bufs=4))
+        psum_one = ctx.enter_context(tc.psum_pool(name="psum_one", bufs=1))
+        ctx.enter_context(tc.manual_schedule())
+
+        chunks = {}
+
+        def token_rows(dram, c):
+            return dram[c * K_PASS : (c + 1) * K_PASS, :].rearrange("(p j) f -> p j f", j=PACK)
+
+        def side_by_side(grouped, rows):
+            return (
+                grouped.rearrange("p (c i) j -> p c j i", i=4),
+                rows.rearrange("p j (c i) -> p c j i", i=4),
+            )
+
+        def load(c):
+            x_sb = inputs.tile([P, PACK, D], BF16)
+            nc.sync.dma_start(out=x_sb[:], in_=token_rows(x_pred, c))
+            gate_sb = inputs.tile([P, PACK, H], BF16)
+            nc.sync.dma_start(out=gate_sb[:], in_=token_rows(gate_pre, c))
+            err_sb = err_in.tile([P, PACK, D], BF16)
+            nc.sync.dma_start(out=err_sb[:], in_=token_rows(err, c))
+            up_sb = inputs.tile([P, PACK, H], BF16)
+            nc.sync.dma_start(out=up_sb[:], in_=token_rows(up_pre, c))
+            chunks[c] = {"gate_sb": gate_sb, "err_sb": err_sb, "x_sb": x_sb, "up_sb": up_sb}
+
+        def transpose_err(c):
+            t = chunks[c]
+            err_words = t["err_sb"][:].bitcast(F32)
+            for pair in range(PACK // 2):
+                err_t = psum_t.tile([P, 2, 2, P], F32, tag="err_t")
+                for jj in range(2):
+                    for u in range(2):
+                        nc.tensor.transpose(
+                            err_t[:, jj, u, :],
+                            err_words[:, 2 * pair + jj, u::2],
+                            ident[:],
+                        )
+                t["err_t", pair] = err_t
+            for j in range(PACK):
+                nc.tensor.matmul(
+                    out=gram[:],
+                    lhsT=t["err_sb"][:, j, 0:GRAM],
+                    rhs=t["err_sb"][:, j, 0:GRAM],
+                    start=(c == 0 and j == 0),
+                    stop=(c == N_CHUNKS - 1 and j == PACK - 1),
+                )
+
+        def scalar_regroup_x(c):
+            t = chunks[c]
+            x_grouped = early.tile([P, D, PACK], BF16, align_bytes=64)
+            to_view, from_view = side_by_side(
+                x_grouped[:, 0:X_SHARE, :], t["x_sb"][:, :, 0:X_SHARE]
+            )
+            nc.scalar.copy(out=to_view, in_=from_view)
+            t["x_grouped"] = x_grouped
+
+        def square_err(c):
+            squares = work.tile([P, PACK, D - GRAM], BF16)
+            nc.scalar.activation(
+                out=squares[:],
+                in_=chunks[c]["err_sb"][:, :, GRAM:D],
+                func=ACT.Square,
+                accum_out=sq_sums[:, c : c + 1],
+            )
+
+        def scalar_work(c):
+            if c < N_CHUNKS:
+                t = chunks[c]
+                silu_neg = early.tile([P, H, PACK], F32)
+                nc.scalar.activation(
+                    out=silu_neg[:],
+                    in_=t["gate_sb"][:].rearrange("p j h -> p h j"),
+                    func=ACT.Silu,
+                    scale=-1.0,
+                )
+                tanh_half = early.tile([P, H, PACK], F32)
+                nc.scalar.activation(
+                    out=tanh_half[:],
+                    in_=t["gate_sb"][:].rearrange("p j h -> p h j"),
+                    func=ACT.Tanh,
+                    scale=0.5,
+                )
+                err_grouped = early.tile([P, K_PASS, PACK], BF16, align_bytes=64)
+                grouped_words = err_grouped[:].bitcast(F32)
+                for pair in range(PACK // 2):
+                    nc.scalar.copy(
+                        out=grouped_words[:, 2 * pair * P : 2 * (pair + 1) * P, :].rearrange(
+                            "q (jj p) u -> q jj p u", jj=2
+                        ),
+                        in_=t["err_t", pair][:].rearrange("q jj u p -> q jj p u"),
+                    )
+                t["silu_neg"] = silu_neg
+                t["err_grouped"] = err_grouped
+                t["tanh_half"] = tanh_half
+            if c + 1 < N_CHUNKS:
+                scalar_regroup_x(c + 1)
+            if c >= SQUARES_LATE:
+                square_err(c - SQUARES_LATE)
+
+        def quantise_err(c):
+            t = chunks[c]
+            err_codes = work.tile([P, K_PASS], U32, align_bytes=64)
+            err_scales = work.tile([P, K_PASS], U8, align_bytes=64)
+            nc.vector.quantize_mx(
+                out=err_codes[:].bitcast(FP8X4),
+                scales=err_scales[:],
+                in_=t["err_grouped"][:].rearrange("q n s -> q (n s)"),
+            )
+            t["err_codes"] = err_codes
+            t["err_scales"] = err_scales
+
+        def first_matmul(c):
+            t = chunks[c]
+            dh = psum_one.tile([P, PACK, H], F32)
+            for j in range(PACK):
+                cols = slice(j * P, (j + 1) * P)
+                nc.tensor.matmul_mx(
+                    out=dh[:, j, :],
+                    lhsT=t["err_codes"][:, cols].bitcast(FP8X4),
+                    lhsT_scale=t["err_scales"][:, cols],
+                    rhs=w_codes[:].bitcast(FP8X4),
+                    rhs_scale=w_scales[:],
+                    start=True,
+                    stop=True,
+                )
+            t["dh"] = dh
+
+        def regroup_x(c):
+            t = chunks[c]
+            to_view, from_view = side_by_side(
+                t["x_grouped"][:, X_SHARE:D, :], t["x_sb"][:, :, X_SHARE:D]
+            )
+            nc.vector.tensor_copy(out=to_view, in_=from_view)
+
+        def quantise_x(c):
+            t = chunks[c]
+            x_codes = x_mx.tile([P, D], U32, align_bytes=64)
+            x_scales = x_mx.tile([P, D], U8, align_bytes=64)
+            nc.vector.quantize_mx(
+                out=x_codes[:].bitcast(FP8X4),
+                scales=x_scales[:],
+                in_=t["x_grouped"][:].rearrange("p d j -> p (d j)"),
+            )
+            t["x_codes"] = x_codes
+            t["x_scales"] = x_scales
+
+        def gate_slope(c):
+            t = chunks[c]
+            neg_slope = work.tile([P, H, PACK], F32)
+            nc.vector.scalar_tensor_tensor(
+                out=neg_slope[:],
+                in0=t["silu_neg"][:],
+                scalar=1.0,
+                in1=t["up_sb"][:].rearrange("p j h -> p h j"),
+                op0=ALU.subtract,
+                op1=ALU.mult,
+            )
+            t["neg_slope"] = neg_slope
+
+        def times_sigmoid(c):
+            t = chunks[c]
+            dh_sig2 = work.tile([P, H, PACK], F32)
+            nc.vector.scalar_tensor_tensor(
+                out=dh_sig2[:],
+                in0=t["tanh_half"][:],
+                scalar=1.0,
+                in1=t["dh"][:].rearrange("p j h -> p h j"),
+                op0=ALU.add,
+                op1=ALU.mult,
+            )
+            t["dh_sig2"] = dh_sig2
+            d_grouped = work.tile([P, 2, H, PACK], BF16, align_bytes=64)
+            t["d_grouped"] = d_grouped
+
+        def d_up_val(c):
+            t = chunks[c]
+            nc.vector.scalar_tensor_tensor(
+                out=t["d_grouped"][:, 0],
+                in0=t["dh_sig2"][:],
+                scalar=0.5,
+                in1=t["gate_sb"][:].rearrange("p j h -> p h j"),
+                op0=ALU.mult,
+                op1=ALU.mult,
+            )
+
+        def d_gate_pre(c):
+            t = chunks[c]
+            nc.vector.scalar_tensor_tensor(
+                out=t["d_grouped"][:, 1],
+                in0=t["dh_sig2"][:],
+                scalar=-0.5,
+                in1=t["neg_slope"][:],
+                op0=ALU.mult,
+                op1=ALU.mult,
+            )
+
+        def quantise_d(c):
+            t = chunks[c]
+            d_codes = work.tile([P, 2, H], U32, align_bytes=64)
+            d_scales = work.tile([P, 2, H], U8, align_bytes=64)
+            nc.vector.quantize_mx(
+                out=d_codes[:].rearrange("p o h -> p (o h)").bitcast(FP8X4),
+                scales=d_scales[:].rearrange("p o h -> p (o h)"),
+                in_=t["d_grouped"][:].rearrange("p o h j -> p (o h j)"),
+            )
+            t["d_codes"] = d_codes
+            t["d_scales"] = d_scales
+
+        def second_matmuls(c):
+            t = chunks[c]
+            for o, acc in enumerate((acc_up, acc_gate)):
+                nc.tensor.matmul_mx(
+                    out=acc[:],
+                    lhsT=t["d_codes"][:, o, :].bitcast(FP8X4),
+                    lhsT_scale=t["d_scales"][:, o, :],
+                    rhs=t["x_codes"][:].bitcast(FP8X4),
+                    rhs_scale=t["x_scales"][:],
+                    start=(c == 0),
+                    stop=(c == N_CHUNKS - 1),
+                )
+
+        def gram_diagonal():
+            diagonal = const.tile([P, GRAM], F32)
+            nc.vector.tensor_tensor(out=diagonal[:], in0=gram[:], in1=ident[:], op=ALU.mult)
+            nc.vector.tensor_reduce(
+                out=sq_sums[:, N_CHUNKS : N_CHUNKS + 1],
+                in_=diagonal[:],
+                axis=mybir.AxisListType.X,
+                op=ALU.add,
+            )
+
+        def surprise_gate():
+            total_ps = psum_t.tile([P, N_CHUNKS + 1], F32, tag="err_t")
+            nc.tensor.matmul(
+                out=total_ps[:], lhsT=ones[:], rhs=sq_sums[:, 0 : N_CHUNKS + 1], start=True, stop=True
+            )
+            total_parts = const.tile([P, N_CHUNKS + 1], F32)
+            mag_sq = const.tile([P, 1], F32)
+            nc.scalar.activation(
+                out=total_parts[:],
+                in_=total_ps[:],
+                func=ACT.Copy,
+                scale=1.0 / (N_TOKENS * N_TOKENS),
+                accum_out=mag_sq[:],
+            )
+            mag = const.tile([P, 1], F32)
+            nc.gpsimd.tensor_tensor(out=mag[:], in0=mag_sq[:], in1=half[:], op=ALU.pow)
+            ema = const.tile([P, 1], F32)
+            nc.gpsimd.tensor_scalar(
+                out=ema[:], in0=mag[:], scalar1=0.05, scalar2=0.95, op0=ALU.mult, op1=ALU.add
+            )
+            ema_floor = const.tile([P, 1], F32)
+            nc.gpsimd.tensor_scalar_max(out=ema_floor[:], in0=ema[:], scalar1=1e-8)
+            ema_inv = const.tile([P, 1], F32)
+            nc.gpsimd.tensor_tensor(out=ema_inv[:], in0=ema_floor[:], in1=minus_one[:], op=ALU.pow)
+            ratio = const.tile([P, 1], F32)
+            nc.gpsimd.tensor_tensor(out=ratio[:], in0=mag[:], in1=ema_inv[:], op=ALU.mult)
+            nc.gpsimd.tensor_scalar(
+                out=gain[:],
+                in0=ratio[:],
+                scalar1=3.0,
+                scalar2=1.0 / N_TOKENS,
+                op0=ALU.min,
+                op1=ALU.mult,
+            )
+
+        load(0)
+        w_raw = const.tile([P, PACK, H], BF16)
+        nc.sync.dma_start(out=w_raw[:], in_=W_down.rearrange("(q t) h -> q t h", t=PACK))
+        for c in range(1, SCALAR_AHEAD + LOAD_AHEAD):
+            load(c)
+
+        ident = const.tile([P, P], F32)
+        make_identity(nc, ident[:])
+        ones = const.tile([P, P], F32)
+        nc.gpsimd.memset(ones[:], 1.0)
+        half = const.tile([P, 1], F32)
+        nc.gpsimd.memset(half[:], 0.5)
+        minus_one = const.tile([P, 1], F32)
+        nc.gpsimd.memset(minus_one[:], -1.0)
+        warm = const.tile([P, 1], F32)
+        nc.scalar.activation(out=warm[:], in_=half[:], func=ACT.Silu)
+
+        sq_sums = const.tile([P, N_CHUNKS + 8], F32)
+        gain = const.tile([P, 1], F32)
+        acc_up = psum_one.tile([P, D], F32)
+        acc_gate = psum_one.tile([P, D], F32)
+        gram = psum_one.tile([P, GRAM], F32)
+
+        scalar_regroup_x(0)
+        transpose_err(0)
+        scalar_work(0)
+
+        regroup_x(0)
+        w_grouped = const.tile([P, H, PACK], BF16, align_bytes=64)
+        nc.vector.tensor_copy(out=w_grouped[:], in_=w_raw[:].rearrange("q t h -> q h t"))
+        quantise_x(0)
+        w_codes = const.tile([P, H], U32, align_bytes=64)
+        w_scales = const.tile([P, H], U8, align_bytes=64)
+        nc.vector.quantize_mx(
+            out=w_codes[:].bitcast(FP8X4),
+            scales=w_scales[:],
+            in_=w_grouped[:].rearrange("q h t -> q (h t)"),
+        )
+        for c in range(1, X_AHEAD):
+            regroup_x(c)
+            quantise_x(c)
+        quantise_err(0)
+        first_matmul(0)
+        for c in range(1, SCALAR_AHEAD):
+            transpose_err(c)
+            scalar_work(c)
+
+        for c in range(N_CHUNKS + 1):
+            if c + SCALAR_AHEAD + LOAD_AHEAD < N_CHUNKS:
+                load(c + SCALAR_AHEAD + LOAD_AHEAD)
+            if c >= 1:
+                quantise_d(c - 1)
+                second_matmuls(c - 1)
+            if c < N_CHUNKS:
+                times_sigmoid(c)
+                gate_slope(c)
+            if c + 1 < N_CHUNKS:
+                quantise_err(c + 1)
+                first_matmul(c + 1)
+            if c == N_CHUNKS - 2:
+                surprise_gate()
+            if c + SCALAR_AHEAD < N_CHUNKS:
+                transpose_err(c + SCALAR_AHEAD)
+                scalar_work(c + SCALAR_AHEAD)
+            if c + SCALAR_AHEAD == N_CHUNKS:
+                for late in range(N_CHUNKS - SQUARES_LATE, N_CHUNKS):
+                    square_err(late)
+                gram_diagonal()
+            if c < N_CHUNKS:
+                d_up_val(c)
+            if c + X_AHEAD < N_CHUNKS:
+                regroup_x(c + X_AHEAD)
+            if c < N_CHUNKS:
+                d_gate_pre(c)
+            if c + X_AHEAD < N_CHUNKS:
+                quantise_x(c + X_AHEAD)
+
+        res_up = const.tile([P, D], F32)
+        nc.scalar.activation(out=res_up[:], in_=acc_up[:], func=ACT.Copy, scale=gain[:, 0:1])
+        nc.sync.dma_start(out=out_0, in_=res_up[:])
+        res_gate = const.tile([P, D], F32)
+        nc.vector.tensor_scalar_mul(out=res_gate[:], in0=acc_gate[:], scalar1=gain[:, 0:1])
+        nc.sync.dma_start(out=out_1, in_=res_gate[:])

@@ -27,6 +27,7 @@ X_AHEAD = 2
 LOAD_AHEAD = 2
 SQUARES_LATE = 4
 GRAM = P
+RUN = 4
 X_SHARE = 128
 
 
@@ -54,11 +55,11 @@ def tile_continuummemorysystem_pa_t_kernel(
         def token_rows(dram, c):
             return dram[c * K_PASS : (c + 1) * K_PASS, :].rearrange("(p j) f -> p j f", j=PACK)
 
-        def side_by_side(grouped, rows):
-            return (
-                grouped.rearrange("p (c i) j -> p c j i", i=4),
-                rows.rearrange("p j (c i) -> p c j i", i=4),
-            )
+        def side_by_side(grouped):
+            return grouped.rearrange("p (c i) j -> p c j i", i=RUN)
+
+        def runs_of_tokens(rows):
+            return rows.rearrange("p j (c i) -> p c j i", i=RUN)
 
         def load(c):
             x_sb = inputs.tile([P, PACK, D], BF16)
@@ -96,10 +97,10 @@ def tile_continuummemorysystem_pa_t_kernel(
         def scalar_regroup_x(c):
             t = chunks[c]
             x_grouped = early.tile([P, D, PACK], BF16, align_bytes=64)
-            to_view, from_view = side_by_side(
-                x_grouped[:, 0:X_SHARE, :], t["x_sb"][:, :, 0:X_SHARE]
+            nc.scalar.copy(
+                out=side_by_side(x_grouped[:, 0:X_SHARE, :]),
+                in_=runs_of_tokens(t["x_sb"][:, :, 0:X_SHARE]),
             )
-            nc.scalar.copy(out=to_view, in_=from_view)
             t["x_grouped"] = x_grouped
 
         def square_err(c):
@@ -114,17 +115,17 @@ def tile_continuummemorysystem_pa_t_kernel(
         def scalar_work(c):
             if c < N_CHUNKS:
                 t = chunks[c]
-                silu_neg = early.tile([P, H, PACK], F32)
+                silu_neg = early.tile([P, PACK, H], F32)
                 nc.scalar.activation(
                     out=silu_neg[:],
-                    in_=t["gate_sb"][:].rearrange("p j h -> p h j"),
+                    in_=t["gate_sb"][:],
                     func=ACT.Silu,
                     scale=-1.0,
                 )
-                tanh_half = early.tile([P, H, PACK], F32)
+                tanh_half = early.tile([P, PACK, H], F32)
                 nc.scalar.activation(
                     out=tanh_half[:],
-                    in_=t["gate_sb"][:].rearrange("p j h -> p h j"),
+                    in_=t["gate_sb"][:],
                     func=ACT.Tanh,
                     scale=0.5,
                 )
@@ -175,10 +176,10 @@ def tile_continuummemorysystem_pa_t_kernel(
 
         def regroup_x(c):
             t = chunks[c]
-            to_view, from_view = side_by_side(
-                t["x_grouped"][:, X_SHARE:D, :], t["x_sb"][:, :, X_SHARE:D]
+            nc.vector.tensor_copy(
+                out=side_by_side(t["x_grouped"][:, X_SHARE:D, :]),
+                in_=runs_of_tokens(t["x_sb"][:, :, X_SHARE:D]),
             )
-            nc.vector.tensor_copy(out=to_view, in_=from_view)
 
         def quantise_x(c):
             t = chunks[c]
@@ -194,12 +195,12 @@ def tile_continuummemorysystem_pa_t_kernel(
 
         def gate_slope(c):
             t = chunks[c]
-            neg_slope = work.tile([P, H, PACK], F32)
+            neg_slope = work.tile([P, PACK, H], F32)
             nc.vector.scalar_tensor_tensor(
                 out=neg_slope[:],
                 in0=t["silu_neg"][:],
                 scalar=1.0,
-                in1=t["up_sb"][:].rearrange("p j h -> p h j"),
+                in1=t["up_sb"][:],
                 op0=ALU.subtract,
                 op1=ALU.mult,
             )
@@ -207,12 +208,12 @@ def tile_continuummemorysystem_pa_t_kernel(
 
         def times_sigmoid(c):
             t = chunks[c]
-            dh_sig2 = work.tile([P, H, PACK], F32)
+            dh_sig2 = work.tile([P, PACK, H], F32)
             nc.vector.scalar_tensor_tensor(
                 out=dh_sig2[:],
                 in0=t["tanh_half"][:],
                 scalar=1.0,
-                in1=t["dh"][:].rearrange("p j h -> p h j"),
+                in1=t["dh"][:],
                 op0=ALU.add,
                 op1=ALU.mult,
             )
@@ -222,24 +223,20 @@ def tile_continuummemorysystem_pa_t_kernel(
 
         def d_up_val(c):
             t = chunks[c]
-            nc.vector.scalar_tensor_tensor(
-                out=t["d_grouped"][:, 0],
-                in0=t["dh_sig2"][:],
-                scalar=0.5,
-                in1=t["gate_sb"][:].rearrange("p j h -> p h j"),
-                op0=ALU.mult,
-                op1=ALU.mult,
+            nc.vector.tensor_tensor(
+                out=side_by_side(t["d_grouped"][:, 0]),
+                in0=runs_of_tokens(t["dh_sig2"][:]),
+                in1=runs_of_tokens(t["gate_sb"][:]),
+                op=ALU.mult,
             )
 
         def d_gate_pre(c):
             t = chunks[c]
-            nc.vector.scalar_tensor_tensor(
-                out=t["d_grouped"][:, 1],
-                in0=t["dh_sig2"][:],
-                scalar=-0.5,
-                in1=t["neg_slope"][:],
-                op0=ALU.mult,
-                op1=ALU.mult,
+            nc.vector.tensor_tensor(
+                out=side_by_side(t["d_grouped"][:, 1]),
+                in0=runs_of_tokens(t["dh_sig2"][:]),
+                in1=runs_of_tokens(t["neg_slope"][:]),
+                op=ALU.mult,
             )
 
         def quantise_d(c):
@@ -307,7 +304,7 @@ def tile_continuummemorysystem_pa_t_kernel(
                 out=gain[:],
                 in0=ratio[:],
                 scalar1=3.0,
-                scalar2=1.0 / N_TOKENS,
+                scalar2=0.5 / N_TOKENS,
                 op0=ALU.min,
                 op1=ALU.mult,
             )
@@ -393,5 +390,12 @@ def tile_continuummemorysystem_pa_t_kernel(
         nc.scalar.activation(out=res_up[:], in_=acc_up[:], func=ACT.Copy, scale=gain[:, 0:1])
         nc.sync.dma_start(out=out_0, in_=res_up[:])
         res_gate = const.tile([P, D], F32)
-        nc.vector.tensor_scalar_mul(out=res_gate[:], in0=acc_gate[:], scalar1=gain[:, 0:1])
+        nc.vector.tensor_scalar(
+            out=res_gate[:],
+            in0=acc_gate[:],
+            scalar1=gain[:, 0:1],
+            scalar2=-1.0,
+            op0=ALU.mult,
+            op1=ALU.mult,
+        )
         nc.sync.dma_start(out=out_1, in_=res_gate[:])

@@ -26,7 +26,8 @@ SCALAR_AHEAD = 3
 X_AHEAD = 2
 LOAD_AHEAD = 2
 SQUARES_LATE = 4
-GRAM = P
+GRAM_COLS = 76
+GRAM = 2 * GRAM_COLS
 RUN = 4
 X_SHARE = 128
 
@@ -38,7 +39,7 @@ def tile_continuummemorysystem_pa_t_kernel(
     with ExitStack() as ctx:
         const = ctx.enter_context(tc.tile_pool(name="const", bufs=1))
         inputs = ctx.enter_context(
-            tc.tile_pool(name="inputs", bufs=LOAD_AHEAD + SCALAR_AHEAD + 2)
+            tc.tile_pool(name="inputs", bufs=LOAD_AHEAD + SCALAR_AHEAD + 3)
         )
         err_in = ctx.enter_context(
             tc.tile_pool(name="err_in", bufs=LOAD_AHEAD + SQUARES_LATE + 2)
@@ -61,16 +62,24 @@ def tile_continuummemorysystem_pa_t_kernel(
         def runs_of_tokens(rows):
             return rows.rearrange("p j (c i) -> p c j i", i=RUN)
 
-        def load(c):
+        def load_x(c):
             x_sb = inputs.tile([P, PACK, D], BF16)
             nc.sync.dma_start(out=x_sb[:], in_=token_rows(x_pred, c))
+            chunks[c] = {"x_sb": x_sb}
+
+        def load(c):
+            t = chunks[c]
             gate_sb = inputs.tile([P, PACK, H], BF16)
             nc.sync.dma_start(out=gate_sb[:], in_=token_rows(gate_pre, c))
             err_sb = err_in.tile([P, PACK, D], BF16)
             nc.sync.dma_start(out=err_sb[:], in_=token_rows(err, c))
+            if c + 1 < N_CHUNKS:
+                load_x(c + 1)
             up_sb = inputs.tile([P, PACK, H], BF16)
             nc.sync.dma_start(out=up_sb[:], in_=token_rows(up_pre, c))
-            chunks[c] = {"gate_sb": gate_sb, "err_sb": err_sb, "x_sb": x_sb, "up_sb": up_sb}
+            t["gate_sb"] = gate_sb
+            t["err_sb"] = err_sb
+            t["up_sb"] = up_sb
 
         def transpose_err(c):
             t = chunks[c]
@@ -86,13 +95,15 @@ def tile_continuummemorysystem_pa_t_kernel(
                         )
                 t["err_t", pair] = err_t
             for j in range(PACK):
-                nc.tensor.matmul(
-                    out=gram[:],
-                    lhsT=t["err_sb"][:, j, 0:GRAM],
-                    rhs=t["err_sb"][:, j, 0:GRAM],
-                    start=(c == 0 and j == 0),
-                    stop=(c == N_CHUNKS - 1 and j == PACK - 1),
-                )
+                for half in range(2):
+                    f0 = half * GRAM_COLS
+                    nc.tensor.matmul(
+                        out=gram[:],
+                        lhsT=t["err_sb"][:, j, f0 : f0 + P],
+                        rhs=t["err_sb"][:, j, f0 : f0 + GRAM_COLS],
+                        start=(c == 0 and j == 0 and half == 0),
+                        stop=(c == N_CHUNKS - 1 and j == PACK - 1 and half == 1),
+                    )
 
         def scalar_regroup_x(c):
             t = chunks[c]
@@ -241,23 +252,38 @@ def tile_continuummemorysystem_pa_t_kernel(
 
         def quantise_d(c):
             t = chunks[c]
-            d_codes = work.tile([P, 2, H], U32, align_bytes=64)
-            d_scales = work.tile([P, 2, H], U8, align_bytes=64)
+            d_codes = work.tile([P, 2 * H], U32, align_bytes=64)
+            d_scales = work.tile([P, 2 * H], U8, align_bytes=64)
             nc.vector.quantize_mx(
-                out=d_codes[:].rearrange("p o h -> p (o h)").bitcast(FP8X4),
-                scales=d_scales[:].rearrange("p o h -> p (o h)"),
+                out=d_codes[:].bitcast(FP8X4),
+                scales=d_scales[:],
                 in_=t["d_grouped"][:].rearrange("p o h j -> p (o h j)"),
             )
-            t["d_codes"] = d_codes
-            t["d_scales"] = d_scales
+            t["d_parts"] = [
+                (d_codes[:, o * H : (o + 1) * H], d_scales[:, o * H : (o + 1) * H])
+                for o in range(2)
+            ]
+
+        def quantise_d_apart(c):
+            t = chunks[c]
+            t["d_parts"] = []
+            for o in range(2):
+                part_codes = work.tile([P, H], U32, align_bytes=64, name="part_codes%d" % o)
+                part_scales = work.tile([P, H], U8, align_bytes=64, name="part_scales%d" % o)
+                nc.vector.quantize_mx(
+                    out=part_codes[:].bitcast(FP8X4),
+                    scales=part_scales[:],
+                    in_=t["d_grouped"][:, o].rearrange("p h j -> p (h j)"),
+                )
+                t["d_parts"].append((part_codes[:], part_scales[:]))
 
         def second_matmuls(c):
             t = chunks[c]
-            for o, acc in enumerate((acc_up, acc_gate)):
+            for (d_codes, d_scales), acc in zip(t["d_parts"], (acc_up, acc_gate)):
                 nc.tensor.matmul_mx(
                     out=acc[:],
-                    lhsT=t["d_codes"][:, o, :].bitcast(FP8X4),
-                    lhsT_scale=t["d_scales"][:, o, :],
+                    lhsT=d_codes.bitcast(FP8X4),
+                    lhsT_scale=d_scales,
                     rhs=t["x_codes"][:].bitcast(FP8X4),
                     rhs_scale=t["x_scales"][:],
                     start=(c == 0),
@@ -265,8 +291,10 @@ def tile_continuummemorysystem_pa_t_kernel(
                 )
 
         def gram_diagonal():
-            diagonal = const.tile([P, GRAM], F32)
-            nc.vector.tensor_tensor(out=diagonal[:], in0=gram[:], in1=ident[:], op=ALU.mult)
+            diagonal = const.tile([P, GRAM_COLS], F32)
+            nc.vector.tensor_tensor(
+                out=diagonal[:], in0=gram[:], in1=ident[:, 0:GRAM_COLS], op=ALU.mult
+            )
             nc.vector.tensor_reduce(
                 out=sq_sums[:, N_CHUNKS : N_CHUNKS + 1],
                 in_=diagonal[:],
@@ -309,10 +337,10 @@ def tile_continuummemorysystem_pa_t_kernel(
                 op1=ALU.mult,
             )
 
-        load(0)
         w_raw = const.tile([P, PACK, H], BF16)
         nc.sync.dma_start(out=w_raw[:], in_=W_down.rearrange("(q t) h -> q t h", t=PACK))
-        for c in range(1, SCALAR_AHEAD + LOAD_AHEAD):
+        load_x(0)
+        for c in range(SCALAR_AHEAD + LOAD_AHEAD):
             load(c)
 
         ident = const.tile([P, P], F32)
@@ -330,16 +358,14 @@ def tile_continuummemorysystem_pa_t_kernel(
         gain = const.tile([P, 1], F32)
         acc_up = psum_one.tile([P, D], F32)
         acc_gate = psum_one.tile([P, D], F32)
-        gram = psum_one.tile([P, GRAM], F32)
+        gram = psum_one.tile([P, GRAM_COLS], F32)
 
         scalar_regroup_x(0)
         transpose_err(0)
         scalar_work(0)
 
-        regroup_x(0)
         w_grouped = const.tile([P, H, PACK], BF16, align_bytes=64)
         nc.vector.tensor_copy(out=w_grouped[:], in_=w_raw[:].rearrange("q t h -> q h t"))
-        quantise_x(0)
         w_codes = const.tile([P, H], U32, align_bytes=64)
         w_scales = const.tile([P, H], U8, align_bytes=64)
         nc.vector.quantize_mx(
@@ -347,11 +373,12 @@ def tile_continuummemorysystem_pa_t_kernel(
             scales=w_scales[:],
             in_=w_grouped[:].rearrange("q h t -> q (h t)"),
         )
-        for c in range(1, X_AHEAD):
-            regroup_x(c)
-            quantise_x(c)
+        regroup_x(0)
+        quantise_x(0)
+        regroup_x(1)
         quantise_err(0)
         first_matmul(0)
+        quantise_x(1)
         for c in range(1, SCALAR_AHEAD):
             transpose_err(c)
             scalar_work(c)
@@ -360,7 +387,10 @@ def tile_continuummemorysystem_pa_t_kernel(
             if c + SCALAR_AHEAD + LOAD_AHEAD < N_CHUNKS:
                 load(c + SCALAR_AHEAD + LOAD_AHEAD)
             if c >= 1:
-                quantise_d(c - 1)
+                if c < N_CHUNKS:
+                    quantise_d(c - 1)
+                else:
+                    quantise_d_apart(c - 1)
                 second_matmuls(c - 1)
             if c < N_CHUNKS:
                 times_sigmoid(c)

@@ -29,7 +29,7 @@ SQUARES_LATE = 4
 GRAM_COLS = 76
 GRAM = 2 * GRAM_COLS
 RUN = 4
-X_SHARE = 128
+X_SHARE = 176
 
 
 def tile_continuummemorysystem_pa_t_kernel(

@@ -19,6 +19,7 @@ N_TOKENS = 8192
 D = 512
 H = 128
 N_CHUNKS = N_TOKENS // K_PASS
+ERR, X = 0, 1
 
 FLOPS = 3 * 2 * N_TOKENS * D * H
 
@@ -45,7 +46,8 @@ def tile_continuummemorysystem_pa_t_kernel(
             tc.tile_pool(name="err_in", bufs=LOAD_AHEAD + SQUARES_LATE + 2)
         )
         early = ctx.enter_context(tc.tile_pool(name="early", bufs=SCALAR_AHEAD + 1))
-        x_mx = ctx.enter_context(tc.tile_pool(name="x_mx", bufs=X_AHEAD + 2))
+        to_mx = ctx.enter_context(tc.tile_pool(name="to_mx", bufs=SCALAR_AHEAD + 2))
+        mx = ctx.enter_context(tc.tile_pool(name="mx", bufs=3))
         work = ctx.enter_context(tc.tile_pool(name="work", bufs=2))
         psum_t = ctx.enter_context(tc.psum_pool(name="psum_t", bufs=4))
         psum_one = ctx.enter_context(tc.psum_pool(name="psum_one", bufs=1))
@@ -107,12 +109,12 @@ def tile_continuummemorysystem_pa_t_kernel(
 
         def scalar_regroup_x(c):
             t = chunks[c]
-            x_grouped = early.tile([P, D, PACK], BF16, align_bytes=64)
+            grouped = to_mx.tile([P, 2, D, PACK], BF16, align_bytes=64)
             nc.scalar.copy(
-                out=side_by_side(x_grouped[:, 0:X_SHARE, :]),
+                out=side_by_side(grouped[:, X, 0:X_SHARE, :]),
                 in_=runs_of_tokens(t["x_sb"][:, :, 0:X_SHARE]),
             )
-            t["x_grouped"] = x_grouped
+            t["grouped"] = grouped
 
         def square_err(c):
             squares = work.tile([P, PACK, D - GRAM], BF16)
@@ -140,8 +142,7 @@ def tile_continuummemorysystem_pa_t_kernel(
                     func=ACT.Tanh,
                     scale=0.5,
                 )
-                err_grouped = early.tile([P, K_PASS, PACK], BF16, align_bytes=64)
-                grouped_words = err_grouped[:].bitcast(F32)
+                grouped_words = t["grouped"][:, ERR].bitcast(F32)
                 for pair in range(PACK // 2):
                     nc.scalar.copy(
                         out=grouped_words[:, 2 * pair * P : 2 * (pair + 1) * P, :].rearrange(
@@ -150,24 +151,24 @@ def tile_continuummemorysystem_pa_t_kernel(
                         in_=t["err_t", pair][:].rearrange("q jj u p -> q jj p u"),
                     )
                 t["silu_neg"] = silu_neg
-                t["err_grouped"] = err_grouped
                 t["tanh_half"] = tanh_half
             if c + 1 < N_CHUNKS:
                 scalar_regroup_x(c + 1)
             if c >= SQUARES_LATE:
                 square_err(c - SQUARES_LATE)
 
-        def quantise_err(c):
+        def quantise(c, operands):
             t = chunks[c]
-            err_codes = work.tile([P, K_PASS], U32, align_bytes=64)
-            err_scales = work.tile([P, K_PASS], U8, align_bytes=64)
+            if "codes" not in t:
+                codes = mx.tile([P, 2, D], U32, align_bytes=64)
+                scales = mx.tile([P, 2, D], U8, align_bytes=64)
+                t["codes"] = codes
+                t["scales"] = scales
             nc.vector.quantize_mx(
-                out=err_codes[:].bitcast(FP8X4),
-                scales=err_scales[:],
-                in_=t["err_grouped"][:].rearrange("q n s -> q (n s)"),
+                out=t["codes"][:, operands].rearrange("p o n -> p (o n)").bitcast(FP8X4),
+                scales=t["scales"][:, operands].rearrange("p o n -> p (o n)"),
+                in_=t["grouped"][:, operands].rearrange("p o n s -> p (o n s)"),
             )
-            t["err_codes"] = err_codes
-            t["err_scales"] = err_scales
 
         def first_matmul(c):
             t = chunks[c]
@@ -176,8 +177,8 @@ def tile_continuummemorysystem_pa_t_kernel(
                 cols = slice(j * P, (j + 1) * P)
                 nc.tensor.matmul_mx(
                     out=dh[:, j, :],
-                    lhsT=t["err_codes"][:, cols].bitcast(FP8X4),
-                    lhsT_scale=t["err_scales"][:, cols],
+                    lhsT=t["codes"][:, ERR, cols].bitcast(FP8X4),
+                    lhsT_scale=t["scales"][:, ERR, cols],
                     rhs=w_codes[:].bitcast(FP8X4),
                     rhs_scale=w_scales[:],
                     start=True,
@@ -188,21 +189,9 @@ def tile_continuummemorysystem_pa_t_kernel(
         def regroup_x(c):
             t = chunks[c]
             nc.vector.tensor_copy(
-                out=side_by_side(t["x_grouped"][:, X_SHARE:D, :]),
+                out=side_by_side(t["grouped"][:, X, X_SHARE:D, :]),
                 in_=runs_of_tokens(t["x_sb"][:, :, X_SHARE:D]),
             )
-
-        def quantise_x(c):
-            t = chunks[c]
-            x_codes = x_mx.tile([P, D], U32, align_bytes=64)
-            x_scales = x_mx.tile([P, D], U8, align_bytes=64)
-            nc.vector.quantize_mx(
-                out=x_codes[:].bitcast(FP8X4),
-                scales=x_scales[:],
-                in_=t["x_grouped"][:].rearrange("p d j -> p (d j)"),
-            )
-            t["x_codes"] = x_codes
-            t["x_scales"] = x_scales
 
         def gate_slope(c):
             t = chunks[c]
@@ -284,8 +273,8 @@ def tile_continuummemorysystem_pa_t_kernel(
                     out=acc[:],
                     lhsT=d_codes.bitcast(FP8X4),
                     lhsT_scale=d_scales,
-                    rhs=t["x_codes"][:].bitcast(FP8X4),
-                    rhs_scale=t["x_scales"][:],
+                    rhs=t["codes"][:, X].bitcast(FP8X4),
+                    rhs_scale=t["scales"][:, X],
                     start=(c == 0),
                     stop=(c == N_CHUNKS - 1),
                 )
@@ -322,10 +311,8 @@ def tile_continuummemorysystem_pa_t_kernel(
             nc.gpsimd.tensor_scalar(
                 out=ema[:], in0=mag[:], scalar1=0.05, scalar2=0.95, op0=ALU.mult, op1=ALU.add
             )
-            ema_floor = const.tile([P, 1], F32)
-            nc.gpsimd.tensor_scalar_max(out=ema_floor[:], in0=ema[:], scalar1=1e-8)
             ema_inv = const.tile([P, 1], F32)
-            nc.gpsimd.tensor_tensor(out=ema_inv[:], in0=ema_floor[:], in1=minus_one[:], op=ALU.pow)
+            nc.gpsimd.tensor_tensor(out=ema_inv[:], in0=ema[:], in1=minus_one[:], op=ALU.pow)
             ratio = const.tile([P, 1], F32)
             nc.gpsimd.tensor_tensor(out=ratio[:], in0=mag[:], in1=ema_inv[:], op=ALU.mult)
             nc.gpsimd.tensor_scalar(
@@ -374,11 +361,10 @@ def tile_continuummemorysystem_pa_t_kernel(
             in_=w_grouped[:].rearrange("q h t -> q (h t)"),
         )
         regroup_x(0)
-        quantise_x(0)
+        quantise(0, slice(X, X + 1))
         regroup_x(1)
-        quantise_err(0)
+        quantise(0, slice(ERR, ERR + 1))
         first_matmul(0)
-        quantise_x(1)
         for c in range(1, SCALAR_AHEAD):
             transpose_err(c)
             scalar_work(c)
@@ -386,17 +372,19 @@ def tile_continuummemorysystem_pa_t_kernel(
         for c in range(N_CHUNKS + 1):
             if c + SCALAR_AHEAD + LOAD_AHEAD < N_CHUNKS:
                 load(c + SCALAR_AHEAD + LOAD_AHEAD)
+            if c < N_CHUNKS:
+                gate_slope(c)
+                times_sigmoid(c)
             if c >= 1:
                 if c < N_CHUNKS:
                     quantise_d(c - 1)
                 else:
                     quantise_d_apart(c - 1)
                 second_matmuls(c - 1)
-            if c < N_CHUNKS:
-                times_sigmoid(c)
-                gate_slope(c)
+            if c + X_AHEAD < N_CHUNKS:
+                regroup_x(c + X_AHEAD)
             if c + 1 < N_CHUNKS:
-                quantise_err(c + 1)
+                quantise(c + 1, slice(0, 2))
                 first_matmul(c + 1)
             if c == N_CHUNKS - 2:
                 surprise_gate()
@@ -409,12 +397,8 @@ def tile_continuummemorysystem_pa_t_kernel(
                 gram_diagonal()
             if c < N_CHUNKS:
                 d_up_val(c)
-            if c + X_AHEAD < N_CHUNKS:
-                regroup_x(c + X_AHEAD)
             if c < N_CHUNKS:
                 d_gate_pre(c)
-            if c + X_AHEAD < N_CHUNKS:
-                quantise_x(c + X_AHEAD)
 
         res_up = const.tile([P, D], F32)
         nc.scalar.activation(out=res_up[:], in_=acc_up[:], func=ACT.Copy, scale=gain[:, 0:1])

@@ -27,8 +27,9 @@ SCALAR_AHEAD = 3
 X_AHEAD = 2
 LOAD_AHEAD = 2
 SQUARES_LATE = 4
-GRAM_COLS = 76
-GRAM = 2 * GRAM_COLS
+GRAM_TAIL = 96
+GRAM = D + GRAM_TAIL
+GRAM_PIECES = ((0, P), (D, GRAM_TAIL), (P, P), (2 * P, P), (3 * P, P))
 RUN = 4
 X_SHARE = 176
 
@@ -96,16 +97,15 @@ def tile_continuummemorysystem_pa_t_kernel(
                             ident[:],
                         )
                 t["err_t", pair] = err_t
-            for j in range(PACK):
-                for half in range(2):
-                    f0 = half * GRAM_COLS
-                    nc.tensor.matmul(
-                        out=gram[:],
-                        lhsT=t["err_sb"][:, j, f0 : f0 + P],
-                        rhs=t["err_sb"][:, j, f0 : f0 + GRAM_COLS],
-                        start=(c == 0 and j == 0 and half == 0),
-                        stop=(c == N_CHUNKS - 1 and j == PACK - 1 and half == 1),
-                    )
+            err_row = t["err_sb"][:].rearrange("p j f -> p (j f)")
+            for i, (e0, cols) in enumerate(GRAM_PIECES):
+                nc.tensor.matmul(
+                    out=gram[:, 0:cols],
+                    lhsT=err_row[:, e0 : e0 + P],
+                    rhs=err_row[:, e0 : e0 + cols],
+                    start=(c == 0 and i == 0),
+                    stop=(c == N_CHUNKS - 1 and i == len(GRAM_PIECES) - 1),
+                )
 
         def scalar_regroup_x(c):
             t = chunks[c]
@@ -117,10 +117,10 @@ def tile_continuummemorysystem_pa_t_kernel(
             t["grouped"] = grouped
 
         def square_err(c):
-            squares = work.tile([P, PACK, D - GRAM], BF16)
+            squares = work.tile([P, PACK * D - GRAM], BF16)
             nc.scalar.activation(
                 out=squares[:],
-                in_=chunks[c]["err_sb"][:, :, GRAM:D],
+                in_=chunks[c]["err_sb"][:].rearrange("p j f -> p (j f)")[:, GRAM : PACK * D],
                 func=ACT.Square,
                 accum_out=sq_sums[:, c : c + 1],
             )
@@ -280,9 +280,9 @@ def tile_continuummemorysystem_pa_t_kernel(
                 )
 
         def gram_diagonal():
-            diagonal = const.tile([P, GRAM_COLS], F32)
+            diagonal = const.tile([P, P], F32)
             nc.vector.tensor_tensor(
-                out=diagonal[:], in0=gram[:], in1=ident[:, 0:GRAM_COLS], op=ALU.mult
+                out=diagonal[:], in0=gram[:], in1=ident[:], op=ALU.mult
             )
             nc.vector.tensor_reduce(
                 out=sq_sums[:, N_CHUNKS : N_CHUNKS + 1],
@@ -345,7 +345,7 @@ def tile_continuummemorysystem_pa_t_kernel(
         gain = const.tile([P, 1], F32)
         acc_up = psum_one.tile([P, D], F32)
         acc_gate = psum_one.tile([P, D], F32)
-        gram = psum_one.tile([P, GRAM_COLS], F32)
+        gram = psum_one.tile([P, P], F32)
 
         scalar_regroup_x(0)
         transpose_err(0)

@@ -31,7 +31,9 @@ GRAM_TAIL = 96
 GRAM = D + GRAM_TAIL
 GRAM_PIECES = ((0, P), (D, GRAM_TAIL), (P, P), (2 * P, P), (3 * P, P))
 RUN = 4
-X_SHARE = 176
+X_GPSIMD = 64
+X_SCALAR = 152
+GPSIMD_FROM = SCALAR_AHEAD + 1
 
 
 def tile_continuummemorysystem_pa_t_kernel(
@@ -111,8 +113,8 @@ def tile_continuummemorysystem_pa_t_kernel(
             t = chunks[c]
             grouped = to_mx.tile([P, 2, D, PACK], BF16, align_bytes=64)
             nc.scalar.copy(
-                out=side_by_side(grouped[:, X, 0:X_SHARE, :]),
-                in_=runs_of_tokens(t["x_sb"][:, :, 0:X_SHARE]),
+                out=side_by_side(grouped[:, X, 0:X_SCALAR, :]),
+                in_=runs_of_tokens(t["x_sb"][:, :, 0:X_SCALAR]),
             )
             t["grouped"] = grouped
 
@@ -188,9 +190,30 @@ def tile_continuummemorysystem_pa_t_kernel(
 
         def regroup_x(c):
             t = chunks[c]
+            end = D if c < GPSIMD_FROM else D - X_GPSIMD
             nc.vector.tensor_copy(
-                out=side_by_side(t["grouped"][:, X, X_SHARE:D, :]),
-                in_=runs_of_tokens(t["x_sb"][:, :, X_SHARE:D]),
+                out=side_by_side(t["grouped"][:, X, X_SCALAR:end, :]),
+                in_=runs_of_tokens(t["x_sb"][:, :, X_SCALAR:end]),
+            )
+
+        def gpsimd_regroup_x(c, after):
+            seen = work.tile([P, 1], BF16)
+            nc.gpsimd.tensor_scalar(
+                out=seen[:],
+                in0=chunks[after]["d_grouped"][:, 1, H - 1, PACK - 1 : PACK],
+                scalar1=1.0,
+                scalar2=0.0,
+                op0=ALU.mult,
+                op1=ALU.add,
+            )
+            t = chunks[c]
+            nc.gpsimd.tensor_scalar(
+                out=side_by_side(t["grouped"][:, X, D - X_GPSIMD : D, :]),
+                in0=runs_of_tokens(t["x_sb"][:, :, D - X_GPSIMD : D]),
+                scalar1=1.0,
+                scalar2=0.0,
+                op0=ALU.mult,
+                op1=ALU.add,
             )
 
         def gate_slope(c):
@@ -397,8 +420,9 @@ def tile_continuummemorysystem_pa_t_kernel(
                 gram_diagonal()
             if c < N_CHUNKS:
                 d_up_val(c)
-            if c < N_CHUNKS:
                 d_gate_pre(c)
+            if GPSIMD_FROM <= c + SCALAR_AHEAD + 1 < N_CHUNKS:
+                gpsimd_regroup_x(c + SCALAR_AHEAD + 1, after=c)
 
         res_up = const.tile([P, D], F32)
         nc.scalar.activation(out=res_up[:], in_=acc_up[:], func=ACT.Copy, scale=gain[:, 0:1])

@@ -31,7 +31,7 @@ GRAM_TAIL = 96
 GRAM = D + GRAM_TAIL
 GRAM_PIECES = ((0, P), (D, GRAM_TAIL), (P, P), (2 * P, P), (3 * P, P))
 RUN = 4
-X_GPSIMD = 64
+X_GPSIMD = 72
 X_SCALAR = 152
 GPSIMD_FROM = SCALAR_AHEAD + 1
 
@@ -197,15 +197,7 @@ def tile_continuummemorysystem_pa_t_kernel(
             )
 
         def gpsimd_regroup_x(c, after):
-            seen = work.tile([P, 1], BF16)
-            nc.gpsimd.tensor_scalar(
-                out=seen[:],
-                in0=chunks[after]["d_grouped"][:, 1, H - 1, PACK - 1 : PACK],
-                scalar1=1.0,
-                scalar2=0.0,
-                op0=ALU.mult,
-                op1=ALU.add,
-            )
+            nc.gpsimd.memset(chunks[after]["neg_slope"][:, PACK - 1, H - 1 : H], 0.0)
             t = chunks[c]
             nc.gpsimd.tensor_scalar(
                 out=side_by_side(t["grouped"][:, X, D - X_GPSIMD : D, :]),

@@ -67,24 +67,17 @@ def tile_continuummemorysystem_pa_t_kernel(
         def runs_of_tokens(rows):
             return rows.rearrange("p j (c i) -> p c j i", i=RUN)
 
-        def load_x(c):
-            x_sb = inputs.tile([P, PACK, D], BF16)
-            nc.sync.dma_start(out=x_sb[:], in_=token_rows(x_pred, c))
-            chunks[c] = {"x_sb": x_sb}
-
         def load(c):
-            t = chunks[c]
+            x_sb = inputs.tile([P, PACK, D], BF16)
             gate_sb = inputs.tile([P, PACK, H], BF16)
-            nc.sync.dma_start(out=gate_sb[:], in_=token_rows(gate_pre, c))
             err_sb = err_in.tile([P, PACK, D], BF16)
-            nc.sync.dma_start(out=err_sb[:], in_=token_rows(err, c))
-            if c + 1 < N_CHUNKS:
-                load_x(c + 1)
             up_sb = inputs.tile([P, PACK, H], BF16)
-            nc.sync.dma_start(out=up_sb[:], in_=token_rows(up_pre, c))
-            t["gate_sb"] = gate_sb
-            t["err_sb"] = err_sb
-            t["up_sb"] = up_sb
+            first = [(x_sb, x_pred), (gate_sb, gate_pre)]
+            if c == 0:
+                first.reverse()
+            for tile, dram in first + [(err_sb, err), (up_sb, up_pre)]:
+                nc.sync.dma_start(out=tile[:], in_=token_rows(dram, c))
+            chunks[c] = {"x_sb": x_sb, "gate_sb": gate_sb, "err_sb": err_sb, "up_sb": up_sb}
 
         def transpose_err(c):
             t = chunks[c]
@@ -99,7 +92,9 @@ def tile_continuummemorysystem_pa_t_kernel(
                             ident[:],
                         )
                 t["err_t", pair] = err_t
-            err_row = t["err_sb"][:].rearrange("p j f -> p (j f)")
+
+        def gram_err(c):
+            err_row = chunks[c]["err_sb"][:].rearrange("p j f -> p (j f)")
             for i, (e0, cols) in enumerate(GRAM_PIECES):
                 nc.tensor.matmul(
                     out=gram[:, 0:cols],
@@ -127,37 +122,41 @@ def tile_continuummemorysystem_pa_t_kernel(
                 accum_out=sq_sums[:, c : c + 1],
             )
 
+        def gate_functions(c):
+            t = chunks[c]
+            silu_neg = early.tile([P, PACK, H], F32)
+            nc.scalar.activation(
+                out=silu_neg[:],
+                in_=t["gate_sb"][:],
+                func=ACT.Silu,
+                scale=-1.0,
+            )
+            tanh_half = early.tile([P, PACK, H], F32)
+            nc.scalar.activation(
+                out=tanh_half[:],
+                in_=t["gate_sb"][:],
+                func=ACT.Tanh,
+                scale=0.5,
+            )
+            t["silu_neg"] = silu_neg
+            t["tanh_half"] = tanh_half
+
+        def copy_err(c):
+            t = chunks[c]
+            grouped_words = t["grouped"][:, ERR].bitcast(F32)
+            for pair in range(PACK // 2):
+                nc.scalar.copy(
+                    out=grouped_words[:, 2 * pair * P : 2 * (pair + 1) * P, :].rearrange(
+                        "q (jj p) u -> q jj p u", jj=2
+                    ),
+                    in_=t["err_t", pair][:].rearrange("q jj u p -> q jj p u"),
+                )
+
         def scalar_work(c):
-            if c < N_CHUNKS:
-                t = chunks[c]
-                silu_neg = early.tile([P, PACK, H], F32)
-                nc.scalar.activation(
-                    out=silu_neg[:],
-                    in_=t["gate_sb"][:],
-                    func=ACT.Silu,
-                    scale=-1.0,
-                )
-                tanh_half = early.tile([P, PACK, H], F32)
-                nc.scalar.activation(
-                    out=tanh_half[:],
-                    in_=t["gate_sb"][:],
-                    func=ACT.Tanh,
-                    scale=0.5,
-                )
-                grouped_words = t["grouped"][:, ERR].bitcast(F32)
-                for pair in range(PACK // 2):
-                    nc.scalar.copy(
-                        out=grouped_words[:, 2 * pair * P : 2 * (pair + 1) * P, :].rearrange(
-                            "q (jj p) u -> q jj p u", jj=2
-                        ),
-                        in_=t["err_t", pair][:].rearrange("q jj u p -> q jj p u"),
-                    )
-                t["silu_neg"] = silu_neg
-                t["tanh_half"] = tanh_half
+            gate_functions(c)
+            copy_err(c)
             if c + 1 < N_CHUNKS:
                 scalar_regroup_x(c + 1)
-            if c >= SQUARES_LATE:
-                square_err(c - SQUARES_LATE)
 
         def quantise(c, operands):
             t = chunks[c]
@@ -320,16 +319,14 @@ def tile_continuummemorysystem_pa_t_kernel(
                 scale=1.0 / (N_TOKENS * N_TOKENS),
                 accum_out=mag_sq[:],
             )
-            mag = const.tile([P, 1], F32)
-            nc.gpsimd.tensor_tensor(out=mag[:], in0=mag_sq[:], in1=half[:], op=ALU.pow)
-            ema = const.tile([P, 1], F32)
+            mag_inv = const.tile([P, 1], F32)
+            nc.gpsimd.tensor_tensor(out=mag_inv[:], in0=mag_sq[:], in1=minus_half[:], op=ALU.pow)
+            ratio_inv = const.tile([P, 1], F32)
             nc.gpsimd.tensor_scalar(
-                out=ema[:], in0=mag[:], scalar1=0.05, scalar2=0.95, op0=ALU.mult, op1=ALU.add
+                out=ratio_inv[:], in0=mag_inv[:], scalar1=0.95, scalar2=0.05, op0=ALU.mult, op1=ALU.add
             )
-            ema_inv = const.tile([P, 1], F32)
-            nc.gpsimd.tensor_tensor(out=ema_inv[:], in0=ema[:], in1=minus_one[:], op=ALU.pow)
             ratio = const.tile([P, 1], F32)
-            nc.gpsimd.tensor_tensor(out=ratio[:], in0=mag[:], in1=ema_inv[:], op=ALU.mult)
+            nc.gpsimd.tensor_tensor(out=ratio[:], in0=ratio_inv[:], in1=minus_one[:], op=ALU.pow)
             nc.gpsimd.tensor_scalar(
                 out=gain[:],
                 in0=ratio[:],
@@ -341,20 +338,19 @@ def tile_continuummemorysystem_pa_t_kernel(
 
         w_raw = const.tile([P, PACK, H], BF16)
         nc.sync.dma_start(out=w_raw[:], in_=W_down.rearrange("(q t) h -> q t h", t=PACK))
-        load_x(0)
-        for c in range(SCALAR_AHEAD + LOAD_AHEAD):
+        for c in range(SCALAR_AHEAD + LOAD_AHEAD + 1):
             load(c)
 
         ident = const.tile([P, P], F32)
         make_identity(nc, ident[:])
         ones = const.tile([P, P], F32)
         nc.gpsimd.memset(ones[:], 1.0)
-        half = const.tile([P, 1], F32)
-        nc.gpsimd.memset(half[:], 0.5)
+        minus_half = const.tile([P, 1], F32)
+        nc.gpsimd.memset(minus_half[:], -0.5)
         minus_one = const.tile([P, 1], F32)
         nc.gpsimd.memset(minus_one[:], -1.0)
         warm = const.tile([P, 1], F32)
-        nc.scalar.activation(out=warm[:], in_=half[:], func=ACT.Silu)
+        nc.scalar.activation(out=warm[:], in_=minus_half[:], func=ACT.Silu)
 
         sq_sums = const.tile([P, N_CHUNKS + 8], F32)
         gain = const.tile([P, 1], F32)
@@ -362,9 +358,12 @@ def tile_continuummemorysystem_pa_t_kernel(
         acc_gate = psum_one.tile([P, D], F32)
         gram = psum_one.tile([P, P], F32)
 
+        gate_functions(0)
         scalar_regroup_x(0)
         transpose_err(0)
-        scalar_work(0)
+        gram_err(0)
+        copy_err(0)
+        scalar_regroup_x(1)
 
         w_grouped = const.tile([P, H, PACK], BF16, align_bytes=64)
         nc.vector.tensor_copy(out=w_grouped[:], in_=w_raw[:].rearrange("q t h -> q h t"))
@@ -377,25 +376,39 @@ def tile_continuummemorysystem_pa_t_kernel(
         )
         regroup_x(0)
         quantise(0, slice(X, X + 1))
+        gate_slope(0)
         regroup_x(1)
         quantise(0, slice(ERR, ERR + 1))
         first_matmul(0)
-        for c in range(1, SCALAR_AHEAD):
-            transpose_err(c)
-            scalar_work(c)
+        quantise(1, slice(X, X + 1))
+        times_sigmoid(0)
+        transpose_err(1)
+        gram_err(1)
+        scalar_work(1)
+        regroup_x(2)
+        d_up_val(0)
+        d_gate_pre(0)
+        transpose_err(2)
+        quantise(1, slice(ERR, ERR + 1))
+        first_matmul(1)
+        gram_err(2)
+        scalar_work(2)
+        transpose_err(SCALAR_AHEAD)
+        gram_err(SCALAR_AHEAD)
+        scalar_work(SCALAR_AHEAD)
+        gpsimd_regroup_x(SCALAR_AHEAD + 1, after=0)
 
-        for c in range(N_CHUNKS + 1):
+        for c in range(1, N_CHUNKS + 1):
             if c + SCALAR_AHEAD + LOAD_AHEAD < N_CHUNKS:
                 load(c + SCALAR_AHEAD + LOAD_AHEAD)
             if c < N_CHUNKS:
                 gate_slope(c)
                 times_sigmoid(c)
-            if c >= 1:
-                if c < N_CHUNKS:
-                    quantise_d(c - 1)
-                else:
-                    quantise_d_apart(c - 1)
-                second_matmuls(c - 1)
+            if c < N_CHUNKS:
+                quantise_d(c - 1)
+            else:
+                quantise_d_apart(c - 1)
+            second_matmuls(c - 1)
             if c + X_AHEAD < N_CHUNKS:
                 regroup_x(c + X_AHEAD)
             if c + 1 < N_CHUNKS:
@@ -405,7 +418,10 @@ def tile_continuummemorysystem_pa_t_kernel(
                 surprise_gate()
             if c + SCALAR_AHEAD < N_CHUNKS:
                 transpose_err(c + SCALAR_AHEAD)
+                gram_err(c + SCALAR_AHEAD)
                 scalar_work(c + SCALAR_AHEAD)
+                if c + SCALAR_AHEAD >= SQUARES_LATE:
+                    square_err(c + SCALAR_AHEAD - SQUARES_LATE)
             if c + SCALAR_AHEAD == N_CHUNKS:
                 for late in range(N_CHUNKS - SQUARES_LATE, N_CHUNKS):
                     square_err(late)
@@ -420,12 +436,13 @@ def tile_continuummemorysystem_pa_t_kernel(
         nc.scalar.activation(out=res_up[:], in_=acc_up[:], func=ACT.Copy, scale=gain[:, 0:1])
         nc.sync.dma_start(out=out_0, in_=res_up[:])
         res_gate = const.tile([P, D], F32)
-        nc.vector.tensor_scalar(
-            out=res_gate[:],
-            in0=acc_gate[:],
-            scalar1=gain[:, 0:1],
-            scalar2=-1.0,
-            op0=ALU.mult,
-            op1=ALU.mult,
-        )
-        nc.sync.dma_start(out=out_1, in_=res_gate[:])
+        for half in (slice(0, D // 2), slice(D // 2, D)):
+            nc.vector.tensor_scalar(
+                out=res_gate[:, half],
+                in0=acc_gate[:, half],
+                scalar1=gain[:, 0:1],
+                scalar2=-1.0,
+                op0=ALU.mult,
+                op1=ALU.mult,
+            )
+            nc.sync.dma_start(out=out_1[:, half], in_=res_gate[:, half])

@@ -48,10 +48,12 @@ def tile_continuummemorysystem_pa_t_kernel(
         err_in = ctx.enter_context(
             tc.tile_pool(name="err_in", bufs=LOAD_AHEAD + SQUARES_LATE + 2)
         )
-        early = ctx.enter_context(tc.tile_pool(name="early", bufs=SCALAR_AHEAD + 1))
+        silus = ctx.enter_context(tc.tile_pool(name="silus", bufs=SCALAR_AHEAD + 2))
+        tanhs = ctx.enter_context(tc.tile_pool(name="tanhs", bufs=SCALAR_AHEAD + 1))
         to_mx = ctx.enter_context(tc.tile_pool(name="to_mx", bufs=SCALAR_AHEAD + 2))
         mx = ctx.enter_context(tc.tile_pool(name="mx", bufs=3))
         work = ctx.enter_context(tc.tile_pool(name="work", bufs=2))
+        slopes = ctx.enter_context(tc.tile_pool(name="slopes", bufs=4))
         psum_t = ctx.enter_context(tc.psum_pool(name="psum_t", bufs=4))
         psum_one = ctx.enter_context(tc.psum_pool(name="psum_one", bufs=1))
         ctx.enter_context(tc.manual_schedule())
@@ -114,24 +116,24 @@ def tile_continuummemorysystem_pa_t_kernel(
             t["grouped"] = grouped
 
         def square_err(c):
-            squares = work.tile([P, PACK * D - GRAM], BF16)
+            rest = chunks[c]["err_sb"][:].rearrange("p j f -> p (j f)")[:, GRAM : PACK * D]
             nc.scalar.activation(
-                out=squares[:],
-                in_=chunks[c]["err_sb"][:].rearrange("p j f -> p (j f)")[:, GRAM : PACK * D],
+                out=rest,
+                in_=rest,
                 func=ACT.Square,
                 accum_out=sq_sums[:, c : c + 1],
             )
 
         def gate_functions(c):
             t = chunks[c]
-            silu_neg = early.tile([P, PACK, H], F32)
+            silu_neg = silus.tile([P, PACK, H], F32)
             nc.scalar.activation(
                 out=silu_neg[:],
                 in_=t["gate_sb"][:],
                 func=ACT.Silu,
                 scale=-1.0,
             )
-            tanh_half = early.tile([P, PACK, H], F32)
+            tanh_half = tanhs.tile([P, PACK, H], F32)
             nc.scalar.activation(
                 out=tanh_half[:],
                 in_=t["gate_sb"][:],
@@ -196,7 +198,7 @@ def tile_continuummemorysystem_pa_t_kernel(
             )
 
         def gpsimd_regroup_x(c, after):
-            nc.gpsimd.memset(chunks[after]["neg_slope"][:, PACK - 1, H - 1 : H], 0.0)
+            nc.gpsimd.memset(chunks[after]["dh_sig2"][:, PACK - 1, H - 1 : H], 0.0)
             t = chunks[c]
             nc.gpsimd.tensor_scalar(
                 out=side_by_side(t["grouped"][:, X, D - X_GPSIMD : D, :]),
@@ -209,7 +211,7 @@ def tile_continuummemorysystem_pa_t_kernel(
 
         def gate_slope(c):
             t = chunks[c]
-            neg_slope = work.tile([P, PACK, H], F32)
+            neg_slope = slopes.tile([P, PACK, H], F32)
             nc.vector.scalar_tensor_tensor(
                 out=neg_slope[:],
                 in0=t["silu_neg"][:],
@@ -222,7 +224,7 @@ def tile_continuummemorysystem_pa_t_kernel(
 
         def times_sigmoid(c):
             t = chunks[c]
-            dh_sig2 = work.tile([P, PACK, H], F32)
+            dh_sig2 = slopes.tile([P, PACK, H], F32)
             nc.vector.scalar_tensor_tensor(
                 out=dh_sig2[:],
                 in0=t["tanh_half"][:],
@@ -386,8 +388,8 @@ def tile_continuummemorysystem_pa_t_kernel(
         gram_err(1)
         scalar_work(1)
         regroup_x(2)
-        d_up_val(0)
         d_gate_pre(0)
+        d_up_val(0)
         transpose_err(2)
         quantise(1, slice(ERR, ERR + 1))
         first_matmul(1)
@@ -427,8 +429,8 @@ def tile_continuummemorysystem_pa_t_kernel(
                     square_err(late)
                 gram_diagonal()
             if c < N_CHUNKS:
-                d_up_val(c)
                 d_gate_pre(c)
+                d_up_val(c)
             if GPSIMD_FROM <= c + SCALAR_AHEAD + 1 < N_CHUNKS:
                 gpsimd_regroup_x(c + SCALAR_AHEAD + 1, after=c)
 

@@ -1,7 +1,6 @@
 from contextlib import ExitStack
 
 import concourse.mybir as mybir
-from concourse.masks import make_identity
 
 F32 = mybir.dt.float32
 BF16 = mybir.dt.bfloat16
@@ -12,6 +11,7 @@ ACT = mybir.ActivationFunctionType
 ALU = mybir.AluOpType
 
 P = 128
+BLOCK = 32
 PACK = 4
 K_PASS = P * PACK
 
@@ -32,8 +32,8 @@ GRAM = D + GRAM_TAIL
 GRAM_PIECES = ((0, P), (D, GRAM_TAIL), (P, P), (2 * P, P), (3 * P, P))
 RUN = 4
 X_GPSIMD = 72
-X_SCALAR = 152
-GPSIMD_FROM = SCALAR_AHEAD + 1
+X_SCALAR = 144
+GPSIMD_FROM = SCALAR_AHEAD + 3
 
 
 def tile_continuummemorysystem_pa_t_kernel(
@@ -343,16 +343,27 @@ def tile_continuummemorysystem_pa_t_kernel(
         for c in range(SCALAR_AHEAD + LOAD_AHEAD + 1):
             load(c)
 
-        ident = const.tile([P, P], F32)
-        make_identity(nc, ident[:])
         ones = const.tile([P, P], F32)
-        nc.gpsimd.memset(ones[:], 1.0)
+        nc.vector.memset(ones[:], 1.0)
+        ident = const.tile([P, P], F32)
+        nc.vector.memset(ident[:], 0.0)
+        ramp = const.tile([P, P], F32, align_bytes=64)
+        nc.vector.tensor_tensor_scan(
+            out=ramp[:], data0=ones[:], data1=ones[:], initial=0.0, op0=ALU.mult, op1=ALU.add
+        )
+        ramp_t = const.tile([P, P], F32, align_bytes=64)
+        nc.vector.transpose(out=ramp_t[:], in_=ramp[:])
+        for p0 in range(0, P, BLOCK):
+            block = slice(p0, p0 + BLOCK)
+            nc.vector.tensor_tensor(
+                out=ident[block, block], in0=ramp[block, block], in1=ramp_t[block, block], op=ALU.is_equal
+            )
         minus_half = const.tile([P, 1], F32)
         nc.gpsimd.memset(minus_half[:], -0.5)
         minus_one = const.tile([P, 1], F32)
         nc.gpsimd.memset(minus_one[:], -1.0)
         warm = const.tile([P, 1], F32)
-        nc.scalar.activation(out=warm[:], in_=minus_half[:], func=ACT.Silu)
+        nc.scalar.activation(out=warm[:], in_=ones[:, 0:1], func=ACT.Silu)
 
         sq_sums = const.tile([P, N_CHUNKS + 8], F32)
         gain = const.tile([P, 1], F32)
@@ -398,7 +409,6 @@ def tile_continuummemorysystem_pa_t_kernel(
         transpose_err(SCALAR_AHEAD)
         gram_err(SCALAR_AHEAD)
         scalar_work(SCALAR_AHEAD)
-        gpsimd_regroup_x(SCALAR_AHEAD + 1, after=0)
 
         for c in range(1, N_CHUNKS + 1):
             if c + SCALAR_AHEAD + LOAD_AHEAD < N_CHUNKS:

@@ -19,6 +19,7 @@ N_TOKENS = 8192
 D = 512
 H = 128
 N_CHUNKS = N_TOKENS // K_PASS
+UP, GATE = 0, 1
 ERR, X = 0, 1
 
 FLOPS = 3 * 2 * N_TOKENS * D * H
@@ -201,8 +202,8 @@ def tile_continuummemorysystem_pa_t_kernel(
             nc.gpsimd.memset(chunks[after]["dh_sig2"][:, PACK - 1, H - 1 : H], 0.0)
             t = chunks[c]
             nc.gpsimd.tensor_scalar(
-                out=side_by_side(t["grouped"][:, X, D - X_GPSIMD : D, :]),
-                in0=runs_of_tokens(t["x_sb"][:, :, D - X_GPSIMD : D]),
+                out=t["grouped"][:, X, D - X_GPSIMD : D, :],
+                in0=t["x_sb"][:, :, D - X_GPSIMD : D].rearrange("p j f -> p f j"),
                 scalar1=1.0,
                 scalar2=0.0,
                 op0=ALU.mult,
@@ -240,7 +241,7 @@ def tile_continuummemorysystem_pa_t_kernel(
         def d_up_val(c):
             t = chunks[c]
             nc.vector.tensor_tensor(
-                out=side_by_side(t["d_grouped"][:, 0]),
+                out=side_by_side(t["d_grouped"][:, UP]),
                 in0=runs_of_tokens(t["dh_sig2"][:]),
                 in1=runs_of_tokens(t["gate_sb"][:]),
                 op=ALU.mult,
@@ -249,7 +250,7 @@ def tile_continuummemorysystem_pa_t_kernel(
         def d_gate_pre(c):
             t = chunks[c]
             nc.vector.tensor_tensor(
-                out=side_by_side(t["d_grouped"][:, 1]),
+                out=side_by_side(t["d_grouped"][:, GATE]),
                 in0=runs_of_tokens(t["dh_sig2"][:]),
                 in1=runs_of_tokens(t["neg_slope"][:]),
                 op=ALU.mult,
@@ -264,15 +265,15 @@ def tile_continuummemorysystem_pa_t_kernel(
                 scales=d_scales[:],
                 in_=t["d_grouped"][:].rearrange("p o h j -> p (o h j)"),
             )
-            t["d_parts"] = [
-                (d_codes[:, o * H : (o + 1) * H], d_scales[:, o * H : (o + 1) * H])
-                for o in range(2)
-            ]
+            t["d_parts"] = {
+                o: (d_codes[:, o * H : (o + 1) * H], d_scales[:, o * H : (o + 1) * H])
+                for o in (GATE, UP)
+            }
 
         def quantise_d_apart(c):
             t = chunks[c]
-            t["d_parts"] = []
-            for o in range(2):
+            t["d_parts"] = {}
+            for o in (GATE, UP):
                 part_codes = work.tile([P, H], U32, align_bytes=64, name="part_codes%d" % o)
                 part_scales = work.tile([P, H], U8, align_bytes=64, name="part_scales%d" % o)
                 nc.vector.quantize_mx(
@@ -280,11 +281,13 @@ def tile_continuummemorysystem_pa_t_kernel(
                     scales=part_scales[:],
                     in_=t["d_grouped"][:, o].rearrange("p h j -> p (h j)"),
                 )
-                t["d_parts"].append((part_codes[:], part_scales[:]))
+                t["d_parts"][o] = (part_codes[:], part_scales[:])
 
         def second_matmuls(c):
             t = chunks[c]
-            for (d_codes, d_scales), acc in zip(t["d_parts"], (acc_up, acc_gate)):
+            for o in (GATE, UP):
+                d_codes, d_scales = t["d_parts"][o]
+                acc = (acc_up, acc_gate)[o]
                 nc.tensor.matmul_mx(
                     out=acc[:],
                     lhsT=d_codes.bitcast(FP8X4),
@@ -297,14 +300,14 @@ def tile_continuummemorysystem_pa_t_kernel(
 
         def gram_diagonal():
             diagonal = const.tile([P, P], F32)
-            nc.vector.tensor_tensor(
-                out=diagonal[:], in0=gram[:], in1=ident[:], op=ALU.mult
-            )
-            nc.vector.tensor_reduce(
-                out=sq_sums[:, N_CHUNKS : N_CHUNKS + 1],
-                in_=diagonal[:],
-                axis=mybir.AxisListType.X,
-                op=ALU.add,
+            nc.vector.scalar_tensor_tensor(
+                out=diagonal[:],
+                in0=gram[:],
+                scalar=1.0,
+                in1=ident[:],
+                op0=ALU.mult,
+                op1=ALU.mult,
+                accum_out=sq_sums[:, N_CHUNKS : N_CHUNKS + 1],
             )
 
         def surprise_gate():
@@ -444,17 +447,19 @@ def tile_continuummemorysystem_pa_t_kernel(
             if GPSIMD_FROM <= c + SCALAR_AHEAD + 1 < N_CHUNKS:
                 gpsimd_regroup_x(c + SCALAR_AHEAD + 1, after=c)
 
-        res_up = const.tile([P, D], F32)
-        nc.scalar.activation(out=res_up[:], in_=acc_up[:], func=ACT.Copy, scale=gain[:, 0:1])
-        nc.sync.dma_start(out=out_0, in_=res_up[:])
         res_gate = const.tile([P, D], F32)
+        nc.vector.tensor_scalar(
+            out=res_gate[:],
+            in0=acc_gate[:],
+            scalar1=gain[:, 0:1],
+            scalar2=-1.0,
+            op0=ALU.mult,
+            op1=ALU.mult,
+        )
+        nc.sync.dma_start(out=out_1, in_=res_gate[:])
+        res_up = const.tile([P, D], F32)
         for half in (slice(0, D // 2), slice(D // 2, D)):
-            nc.vector.tensor_scalar(
-                out=res_gate[:, half],
-                in0=acc_gate[:, half],
-                scalar1=gain[:, 0:1],
-                scalar2=-1.0,
-                op0=ALU.mult,
-                op1=ALU.mult,
+            nc.scalar.activation(
+                out=res_up[:, half], in_=acc_up[:, half], func=ACT.Copy, scale=gain[:, 0:1]
             )
-            nc.sync.dma_start(out=out_1[:, half], in_=res_gate[:, half])
+            nc.sync.dma_start(out=out_0[:, half], in_=res_up[:, half])

@@ -33,7 +33,7 @@ GRAM = D + GRAM_TAIL
 GRAM_PIECES = ((0, P), (D, GRAM_TAIL), (P, P), (2 * P, P), (3 * P, P))
 RUN = 4
 X_GPSIMD = 72
-X_SCALAR = 144
+X_SCALAR = 128
 GPSIMD_FROM = SCALAR_AHEAD + 3
 
 
@@ -321,25 +321,16 @@ def tile_continuummemorysystem_pa_t_kernel(
                 out=total_parts[:],
                 in_=total_ps[:],
                 func=ACT.Copy,
-                scale=1.0 / (N_TOKENS * N_TOKENS),
+                scale=1.0 / (0.95 * N_TOKENS) ** 2,
                 accum_out=mag_sq[:],
             )
             mag_inv = const.tile([P, 1], F32)
             nc.gpsimd.tensor_tensor(out=mag_inv[:], in0=mag_sq[:], in1=minus_half[:], op=ALU.pow)
-            ratio_inv = const.tile([P, 1], F32)
+            sg_inv = const.tile([P, 1], F32)
             nc.gpsimd.tensor_scalar(
-                out=ratio_inv[:], in0=mag_inv[:], scalar1=0.95, scalar2=0.05, op0=ALU.mult, op1=ALU.add
+                out=sg_inv[:], in0=mag_inv[:], scalar1=0.05, scalar2=1.0 / 3.0, op0=ALU.add, op1=ALU.max
             )
-            ratio = const.tile([P, 1], F32)
-            nc.gpsimd.tensor_tensor(out=ratio[:], in0=ratio_inv[:], in1=minus_one[:], op=ALU.pow)
-            nc.gpsimd.tensor_scalar(
-                out=gain[:],
-                in0=ratio[:],
-                scalar1=3.0,
-                scalar2=0.5 / N_TOKENS,
-                op0=ALU.min,
-                op1=ALU.mult,
-            )
+            nc.gpsimd.tensor_tensor(out=gain[:], in0=sg_inv[:], in1=minus_one[:], op=ALU.pow)
 
         w_raw = const.tile([P, PACK, H], BF16)
         nc.sync.dma_start(out=w_raw[:], in_=W_down.rearrange("(q t) h -> q t h", t=PACK))
@@ -382,7 +373,9 @@ def tile_continuummemorysystem_pa_t_kernel(
         scalar_regroup_x(1)
 
         w_grouped = const.tile([P, H, PACK], BF16, align_bytes=64)
-        nc.vector.tensor_copy(out=w_grouped[:], in_=w_raw[:].rearrange("q t h -> q h t"))
+        nc.vector.tensor_scalar_mul(
+            w_grouped[:], w_raw[:].rearrange("q t h -> q h t"), 0.5 / N_TOKENS
+        )
         w_codes = const.tile([P, H], U32, align_bytes=64)
         w_scales = const.tile([P, H], U8, align_bytes=64)
         nc.vector.quantize_mx(

from contextlib import ExitStack

import concourse.mybir as mybir

F32 = mybir.dt.float32
BF16 = mybir.dt.bfloat16
U32 = mybir.dt.uint32
U8 = mybir.dt.uint8
FP8X4 = mybir.dt.float8_e4m3fn_x4
ACT = mybir.ActivationFunctionType
ALU = mybir.AluOpType

P = 128
BLOCK = 32
PACK = 4
K_PASS = P * PACK

N_TOKENS = 8192
D = 512
H = 128
N_CHUNKS = N_TOKENS // K_PASS
UP, GATE = 0, 1
ERR, X = 0, 1

FLOPS = 3 * 2 * N_TOKENS * D * H

SCALAR_AHEAD = 3
X_AHEAD = 2
LOAD_AHEAD = 2
SQUARES_LATE = 4
GRAM_TAIL = 96
GRAM = D + GRAM_TAIL
GRAM_PIECES = ((0, P), (D, GRAM_TAIL), (P, P), (2 * P, P), (3 * P, P))
RUN = 4
X_GPSIMD = 72
X_SCALAR = 128
GPSIMD_FROM = SCALAR_AHEAD + 3


def tile_continuummemorysystem_pa_t_kernel(
    tc, err, W_down, gate_pre, up_pre, x_pred, out_0, out_1
):
    nc = tc.nc
    with ExitStack() as ctx:
        const = ctx.enter_context(tc.tile_pool(name="const", bufs=1))
        inputs = ctx.enter_context(
            tc.tile_pool(name="inputs", bufs=LOAD_AHEAD + SCALAR_AHEAD + 3)
        )
        err_in = ctx.enter_context(
            tc.tile_pool(name="err_in", bufs=LOAD_AHEAD + SQUARES_LATE + 2)
        )
        silus = ctx.enter_context(tc.tile_pool(name="silus", bufs=SCALAR_AHEAD + 2))
        tanhs = ctx.enter_context(tc.tile_pool(name="tanhs", bufs=SCALAR_AHEAD + 1))
        to_mx = ctx.enter_context(tc.tile_pool(name="to_mx", bufs=SCALAR_AHEAD + 2))
        mx = ctx.enter_context(tc.tile_pool(name="mx", bufs=3))
        work = ctx.enter_context(tc.tile_pool(name="work", bufs=2))
        slopes = ctx.enter_context(tc.tile_pool(name="slopes", bufs=4))
        psum_t = ctx.enter_context(tc.psum_pool(name="psum_t", bufs=4))
        psum_one = ctx.enter_context(tc.psum_pool(name="psum_one", bufs=1))
        ctx.enter_context(tc.manual_schedule())

        chunks = {}

        def token_rows(dram, c):
            return dram[c * K_PASS : (c + 1) * K_PASS, :].rearrange("(p j) f -> p j f", j=PACK)

        def side_by_side(grouped):
            return grouped.rearrange("p (c i) j -> p c j i", i=RUN)

        def runs_of_tokens(rows):
            return rows.rearrange("p j (c i) -> p c j i", i=RUN)

        def load(c):
            x_sb = inputs.tile([P, PACK, D], BF16)
            gate_sb = inputs.tile([P, PACK, H], BF16)
            err_sb = err_in.tile([P, PACK, D], BF16)
            up_sb = inputs.tile([P, PACK, H], BF16)
            first = [(x_sb, x_pred), (gate_sb, gate_pre)]
            if c == 0:
                first.reverse()
            for tile, dram in first + [(err_sb, err), (up_sb, up_pre)]:
                nc.sync.dma_start(out=tile[:], in_=token_rows(dram, c))
            chunks[c] = {"x_sb": x_sb, "gate_sb": gate_sb, "err_sb": err_sb, "up_sb": up_sb}

        def transpose_err(c):
            t = chunks[c]
            err_words = t["err_sb"][:].bitcast(F32)
            for pair in range(PACK // 2):
                err_t = psum_t.tile([P, 2, 2, P], F32, tag="err_t")
                for jj in range(2):
                    for u in range(2):
                        nc.tensor.transpose(
                            err_t[:, jj, u, :],
                            err_words[:, 2 * pair + jj, u::2],
                            ident[:],
                        )
                t["err_t", pair] = err_t

        def gram_err(c):
            err_row = chunks[c]["err_sb"][:].rearrange("p j f -> p (j f)")
            for i, (e0, cols) in enumerate(GRAM_PIECES):
                nc.tensor.matmul(
                    out=gram[:, 0:cols],
                    lhsT=err_row[:, e0 : e0 + P],
                    rhs=err_row[:, e0 : e0 + cols],
                    start=(c == 0 and i == 0),
                    stop=(c == N_CHUNKS - 1 and i == len(GRAM_PIECES) - 1),
                )

        def scalar_regroup_x(c):
            t = chunks[c]
            grouped = to_mx.tile([P, 2, D, PACK], BF16, align_bytes=64)
            nc.scalar.copy(
                out=side_by_side(grouped[:, X, 0:X_SCALAR, :]),
                in_=runs_of_tokens(t["x_sb"][:, :, 0:X_SCALAR]),
            )
            t["grouped"] = grouped

        def square_err(c):
            rest = chunks[c]["err_sb"][:].rearrange("p j f -> p (j f)")[:, GRAM : PACK * D]
            nc.scalar.activation(
                out=rest,
                in_=rest,
                func=ACT.Square,
                accum_out=sq_sums[:, c : c + 1],
            )

        def gate_functions(c):
            t = chunks[c]
            silu_neg = silus.tile([P, PACK, H], F32)
            nc.scalar.activation(
                out=silu_neg[:],
                in_=t["gate_sb"][:],
                func=ACT.Silu,
                scale=-1.0,
            )
            tanh_half = tanhs.tile([P, PACK, H], F32)
            nc.scalar.activation(
                out=tanh_half[:],
                in_=t["gate_sb"][:],
                func=ACT.Tanh,
                scale=0.5,
            )
            t["silu_neg"] = silu_neg
            t["tanh_half"] = tanh_half

        def copy_err(c):
            t = chunks[c]
            grouped_words = t["grouped"][:, ERR].bitcast(F32)
            for pair in range(PACK // 2):
                nc.scalar.copy(
                    out=grouped_words[:, 2 * pair * P : 2 * (pair + 1) * P, :].rearrange(
                        "q (jj p) u -> q jj p u", jj=2
                    ),
                    in_=t["err_t", pair][:].rearrange("q jj u p -> q jj p u"),
                )

        def scalar_work(c):
            gate_functions(c)
            copy_err(c)
            if c + 1 < N_CHUNKS:
                scalar_regroup_x(c + 1)

        def quantise(c, operands):
            t = chunks[c]
            if "codes" not in t:
                codes = mx.tile([P, 2, D], U32, align_bytes=64)
                scales = mx.tile([P, 2, D], U8, align_bytes=64)
                t["codes"] = codes
                t["scales"] = scales
            nc.vector.quantize_mx(
                out=t["codes"][:, operands].rearrange("p o n -> p (o n)").bitcast(FP8X4),
                scales=t["scales"][:, operands].rearrange("p o n -> p (o n)"),
                in_=t["grouped"][:, operands].rearrange("p o n s -> p (o n s)"),
            )

        def first_matmul(c):
            t = chunks[c]
            dh = psum_one.tile([P, PACK, H], F32)
            for j in range(PACK):
                cols = slice(j * P, (j + 1) * P)
                nc.tensor.matmul_mx(
                    out=dh[:, j, :],
                    lhsT=t["codes"][:, ERR, cols].bitcast(FP8X4),
                    lhsT_scale=t["scales"][:, ERR, cols],
                    rhs=w_codes[:].bitcast(FP8X4),
                    rhs_scale=w_scales[:],
                    start=True,
                    stop=True,
                )
            t["dh"] = dh

        def regroup_x(c):
            t = chunks[c]
            end = D if c < GPSIMD_FROM else D - X_GPSIMD
            nc.vector.tensor_copy(
                out=side_by_side(t["grouped"][:, X, X_SCALAR:end, :]),
                in_=runs_of_tokens(t["x_sb"][:, :, X_SCALAR:end]),
            )

        def gpsimd_regroup_x(c, after):
            nc.gpsimd.memset(chunks[after]["dh_sig2"][:, PACK - 1, H - 1 : H], 0.0)
            t = chunks[c]
            nc.gpsimd.tensor_scalar(
                out=t["grouped"][:, X, D - X_GPSIMD : D, :],
                in0=t["x_sb"][:, :, D - X_GPSIMD : D].rearrange("p j f -> p f j"),
                scalar1=1.0,
                scalar2=0.0,
                op0=ALU.mult,
                op1=ALU.add,
            )

        def gate_slope(c):
            t = chunks[c]
            neg_slope = slopes.tile([P, PACK, H], F32)
            nc.vector.scalar_tensor_tensor(
                out=neg_slope[:],
                in0=t["silu_neg"][:],
                scalar=1.0,
                in1=t["up_sb"][:],
                op0=ALU.subtract,
                op1=ALU.mult,
            )
            t["neg_slope"] = neg_slope

        def times_sigmoid(c):
            t = chunks[c]
            dh_sig2 = slopes.tile([P, PACK, H], F32)
            nc.vector.scalar_tensor_tensor(
                out=dh_sig2[:],
                in0=t["tanh_half"][:],
                scalar=1.0,
                in1=t["dh"][:],
                op0=ALU.add,
                op1=ALU.mult,
            )
            t["dh_sig2"] = dh_sig2
            d_grouped = work.tile([P, 2, H, PACK], BF16, align_bytes=64)
            t["d_grouped"] = d_grouped

        def d_up_val(c):
            t = chunks[c]
            nc.vector.tensor_tensor(
                out=side_by_side(t["d_grouped"][:, UP]),
                in0=runs_of_tokens(t["dh_sig2"][:]),
                in1=runs_of_tokens(t["gate_sb"][:]),
                op=ALU.mult,
            )

        def d_gate_pre(c):
            t = chunks[c]
            nc.vector.tensor_tensor(
                out=side_by_side(t["d_grouped"][:, GATE]),
                in0=runs_of_tokens(t["dh_sig2"][:]),
                in1=runs_of_tokens(t["neg_slope"][:]),
                op=ALU.mult,
            )

        def quantise_d(c):
            t = chunks[c]
            d_codes = work.tile([P, 2 * H], U32, align_bytes=64)
            d_scales = work.tile([P, 2 * H], U8, align_bytes=64)
            nc.vector.quantize_mx(
                out=d_codes[:].bitcast(FP8X4),
                scales=d_scales[:],
                in_=t["d_grouped"][:].rearrange("p o h j -> p (o h j)"),
            )
            t["d_parts"] = {
                o: (d_codes[:, o * H : (o + 1) * H], d_scales[:, o * H : (o + 1) * H])
                for o in (GATE, UP)
            }

        def quantise_d_apart(c):
            t = chunks[c]
            t["d_parts"] = {}
            for o in (GATE, UP):
                part_codes = work.tile([P, H], U32, align_bytes=64, name="part_codes%d" % o)
                part_scales = work.tile([P, H], U8, align_bytes=64, name="part_scales%d" % o)
                nc.vector.quantize_mx(
                    out=part_codes[:].bitcast(FP8X4),
                    scales=part_scales[:],
                    in_=t["d_grouped"][:, o].rearrange("p h j -> p (h j)"),
                )
                t["d_parts"][o] = (part_codes[:], part_scales[:])

        def second_matmuls(c):
            t = chunks[c]
            for o in (GATE, UP):
                d_codes, d_scales = t["d_parts"][o]
                acc = (acc_up, acc_gate)[o]
                nc.tensor.matmul_mx(
                    out=acc[:],
                    lhsT=d_codes.bitcast(FP8X4),
                    lhsT_scale=d_scales,
                    rhs=t["codes"][:, X].bitcast(FP8X4),
                    rhs_scale=t["scales"][:, X],
                    start=(c == 0),
                    stop=(c == N_CHUNKS - 1),
                )

        def gram_diagonal():
            diagonal = const.tile([P, P], F32)
            nc.vector.scalar_tensor_tensor(
                out=diagonal[:],
                in0=gram[:],
                scalar=1.0,
                in1=ident[:],
                op0=ALU.mult,
                op1=ALU.mult,
                accum_out=sq_sums[:, N_CHUNKS : N_CHUNKS + 1],
            )

        def surprise_gate():
            total_ps = psum_t.tile([P, N_CHUNKS + 1], F32, tag="err_t")
            nc.tensor.matmul(
                out=total_ps[:], lhsT=ones[:], rhs=sq_sums[:, 0 : N_CHUNKS + 1], start=True, stop=True
            )
            total_parts = const.tile([P, N_CHUNKS + 1], F32)
            mag_sq = const.tile([P, 1], F32)
            nc.scalar.activation(
                out=total_parts[:],
                in_=total_ps[:],
                func=ACT.Copy,
                scale=1.0 / (0.95 * N_TOKENS) ** 2,
                accum_out=mag_sq[:],
            )
            mag_inv = const.tile([P, 1], F32)
            nc.gpsimd.tensor_tensor(out=mag_inv[:], in0=mag_sq[:], in1=minus_half[:], op=ALU.pow)
            sg_inv = const.tile([P, 1], F32)
            nc.gpsimd.tensor_scalar(
                out=sg_inv[:], in0=mag_inv[:], scalar1=0.05, scalar2=1.0 / 3.0, op0=ALU.add, op1=ALU.max
            )
            nc.gpsimd.tensor_tensor(out=gain[:], in0=sg_inv[:], in1=minus_one[:], op=ALU.pow)

        w_raw = const.tile([P, PACK, H], BF16)
        nc.sync.dma_start(out=w_raw[:], in_=W_down.rearrange("(q t) h -> q t h", t=PACK))
        for c in range(SCALAR_AHEAD + LOAD_AHEAD + 1):
            load(c)

        ones = const.tile([P, P], F32)
        nc.vector.memset(ones[:], 1.0)
        ident = const.tile([P, P], F32)
        nc.vector.memset(ident[:], 0.0)
        ramp = const.tile([P, P], F32, align_bytes=64)
        nc.vector.tensor_tensor_scan(
            out=ramp[:], data0=ones[:], data1=ones[:], initial=0.0, op0=ALU.mult, op1=ALU.add
        )
        ramp_t = const.tile([P, P], F32, align_bytes=64)
        nc.vector.transpose(out=ramp_t[:], in_=ramp[:])
        for p0 in range(0, P, BLOCK):
            block = slice(p0, p0 + BLOCK)
            nc.vector.tensor_tensor(
                out=ident[block, block], in0=ramp[block, block], in1=ramp_t[block, block], op=ALU.is_equal
            )
        minus_half = const.tile([P, 1], F32)
        nc.gpsimd.memset(minus_half[:], -0.5)
        minus_one = const.tile([P, 1], F32)
        nc.gpsimd.memset(minus_one[:], -1.0)
        warm = const.tile([P, 1], F32)
        nc.scalar.activation(out=warm[:], in_=ones[:, 0:1], func=ACT.Silu)

        sq_sums = const.tile([P, N_CHUNKS + 8], F32)
        gain = const.tile([P, 1], F32)
        acc_up = psum_one.tile([P, D], F32)
        acc_gate = psum_one.tile([P, D], F32)
        gram = psum_one.tile([P, P], F32)

        gate_functions(0)
        scalar_regroup_x(0)
        transpose_err(0)
        gram_err(0)
        copy_err(0)
        scalar_regroup_x(1)

        w_grouped = const.tile([P, H, PACK], BF16, align_bytes=64)
        nc.vector.tensor_scalar_mul(
            w_grouped[:], w_raw[:].rearrange("q t h -> q h t"), 0.5 / N_TOKENS
        )
        w_codes = const.tile([P, H], U32, align_bytes=64)
        w_scales = const.tile([P, H], U8, align_bytes=64)
        nc.vector.quantize_mx(
            out=w_codes[:].bitcast(FP8X4),
            scales=w_scales[:],
            in_=w_grouped[:].rearrange("q h t -> q (h t)"),
        )
        regroup_x(0)
        quantise(0, slice(X, X + 1))
        gate_slope(0)
        regroup_x(1)
        quantise(0, slice(ERR, ERR + 1))
        first_matmul(0)
        quantise(1, slice(X, X + 1))
        times_sigmoid(0)
        transpose_err(1)
        gram_err(1)
        scalar_work(1)
        regroup_x(2)
        d_gate_pre(0)
        d_up_val(0)
        transpose_err(2)
        quantise(1, slice(ERR, ERR + 1))
        first_matmul(1)
        gram_err(2)
        scalar_work(2)
        transpose_err(SCALAR_AHEAD)
        gram_err(SCALAR_AHEAD)
        scalar_work(SCALAR_AHEAD)

        for c in range(1, N_CHUNKS + 1):
            if c + SCALAR_AHEAD + LOAD_AHEAD < N_CHUNKS:
                load(c + SCALAR_AHEAD + LOAD_AHEAD)
            if c < N_CHUNKS:
                gate_slope(c)
                times_sigmoid(c)
            if c < N_CHUNKS:
                quantise_d(c - 1)
            else:
                quantise_d_apart(c - 1)
            second_matmuls(c - 1)
            if c + X_AHEAD < N_CHUNKS:
                regroup_x(c + X_AHEAD)
            if c + 1 < N_CHUNKS:
                quantise(c + 1, slice(0, 2))
                first_matmul(c + 1)
            if c == N_CHUNKS - 2:
                surprise_gate()
            if c + SCALAR_AHEAD < N_CHUNKS:
                transpose_err(c + SCALAR_AHEAD)
                gram_err(c + SCALAR_AHEAD)
                scalar_work(c + SCALAR_AHEAD)
                if c + SCALAR_AHEAD >= SQUARES_LATE:
                    square_err(c + SCALAR_AHEAD - SQUARES_LATE)
            if c + SCALAR_AHEAD == N_CHUNKS:
                for late in range(N_CHUNKS - SQUARES_LATE, N_CHUNKS):
                    square_err(late)
                gram_diagonal()
            if c < N_CHUNKS:
                d_gate_pre(c)
                d_up_val(c)
            if GPSIMD_FROM <= c + SCALAR_AHEAD + 1 < N_CHUNKS:
                gpsimd_regroup_x(c + SCALAR_AHEAD + 1, after=c)

        res_gate = const.tile([P, D], F32)
        nc.vector.tensor_scalar(
            out=res_gate[:],
            in0=acc_gate[:],
            scalar1=gain[:, 0:1],
            scalar2=-1.0,
            op0=ALU.mult,
            op1=ALU.mult,
        )
        nc.sync.dma_start(out=out_1, in_=res_gate[:])
        res_up = const.tile([P, D], F32)
        for half in (slice(0, D // 2), slice(D // 2, D)):
            nc.scalar.activation(
                out=res_up[:, half], in_=acc_up[:, half], func=ACT.Copy, scale=gain[:, 0:1]
            )
            nc.sync.dma_start(out=out_0[:, half], in_=res_up[:, half])
